import numpy as np
import ml_dtypes


def mxq(x, axis, fmt="e4m3"):
    dtype, down = {"e4m3": (ml_dtypes.float8_e4m3fn, 7), "e5m2": (ml_dtypes.float8_e5m2, 14)}[fmt]
    v = np.moveaxis(np.asarray(x, np.float32).astype(ml_dtypes.bfloat16).astype(np.float64), axis, -1)
    blocks = v.reshape(v.shape[:-1] + (-1, 32))
    amax = np.abs(blocks).max(-1, keepdims=True)
    byte = np.maximum(np.where(amax > 0, np.frexp(amax)[1] - 1 + 127, 0) - down, 1)
    scale = np.exp2(byte - 127.0)
    codes = (blocks / scale).astype(np.float32).astype(dtype).astype(np.float64)
    return np.moveaxis((codes * scale).reshape(v.shape), -1, axis)


WIDE = False


def mx_kscale(k):
    if not WIDE:
        return np.ones(k)
    levels = np.array([10, -10, 5, -5, 0])
    if k % 512:
        return np.exp2(np.random.permutation(np.resize(levels, k // 32))).repeat(32)
    a = np.empty((k // 512, 16))
    for p in range(k // 512):
        a[p, :8] = np.random.permutation(np.resize(levels, 8))
        for g in range(8):
            far = levels[np.abs(levels - a[p, g]) >= 10]
            a[p, g + 8] = far[np.random.randint(len(far))]
    return np.exp2(a.ravel()).repeat(32)


BF16 = ml_dtypes.bfloat16


def bf(x):
    return np.asarray(x, np.float32).astype(BF16)


def f64(x):
    return np.asarray(x).astype(np.float64)


B, S, D, H, QL, KVL, RD, ND, VD = 2, 1536, 4096, 16, 3072, 512, 128, 64, 128
QHD = ND + RD
ROPE_THETA, ROPE_RATIO = 10000.0, 1.0


def rope_tables(seq_len):
    half = RD // 2
    inv_freq = ROPE_RATIO / (ROPE_THETA ** (np.arange(half) * 2.0 / RD))
    freqs = np.arange(seq_len)[:, None] * inv_freq[None, :]
    return np.cos(freqs), np.sin(freqs)


def apply_rope(x, cos, sin):
    x_even = x[..., 0::2]
    x_odd = x[..., 1::2]
    r_even = x_even * cos - x_odd * sin
    r_odd = x_odd * cos + x_even * sin
    return np.stack([r_even, r_odd], axis=-1).reshape(x.shape)


def setup_inputs():
    s, t = mx_kscale(D), mx_kscale(QL)
    return {"hidden_states": bf(np.random.standard_normal((B, S, D)) * s),
            "Wqa": bf(np.random.standard_normal((D, QL)) / np.sqrt(D) / s[:, None] * t),
            "Wqb": bf(np.random.standard_normal((QL, H * QHD)) / np.sqrt(QL) / t[:, None])}


def reference(hidden_states, Wqa, Wqb):
    q_latent = mxq(f64(hidden_states), 2, "e4m3") @ mxq(f64(Wqa), 0, "e4m3")
    q = (mxq(q_latent, 2, "e4m3") @ mxq(f64(Wqb), 0, "e4m3")).reshape(B, S, H, QHD)
    q = q.transpose(0, 2, 1, 3)
    q_nope, q_pe = q[..., :ND], q[..., ND:]
    cos, sin = rope_tables(S)
    q_pe = apply_rope(q_pe, cos, sin)
    return np.concatenate([q_nope, q_pe], axis=-1)

@@ -1,0 +1,497 @@
+from contextlib import ExitStack
+import math
+
+import concourse.mybir as mybir
+from concourse.masks import make_identity
+
+F32 = mybir.dt.float32
+BF16 = mybir.dt.bfloat16
+U32 = mybir.dt.uint32
+U8 = mybir.dt.uint8
+I32 = mybir.dt.int32
+FP8X4 = mybir.dt.float8_e4m3fn_x4
+ALU = mybir.AluOpType
+ACT = mybir.ActivationFunctionType
+
+P = 128
+TOKENS = 3072
+SEQ = 1536
+D_IN = 4096
+LATENT = 3072
+HEADS = 16
+HEAD = 192
+NOPE = 64
+FLOPS = 2 * TOKENS * D_IN * LATENT + 2 * TOKENS * LATENT * HEADS * HEAD
+
+KIB = 1024
+PI = 3.141592653589793
+QLC = 0
+QLPL = 60
+XC = 66
+XPL = 162
+WCB = 168
+WPLB = 184
+WCA = 185
+WPLA = 201
+WRAW = 202
+WGRP = 210
+QGRP = 218
+QST = 222
+TAB = 230
+WRAWH = 12
+XRAW = 24
+XGRP = 48
+IDENT = 230
+WPL0 = 231
+FRQ = 36
+TMP = 37
+BRAW = 185
+RGRP = 203
+NGRP = 211
+BPL0 = 215
+OUTT = 156
+BPL1 = 174
+RTMP = 177
+
+
+def round_bits(x, bits):
+    if x == 0.0:
+        return 0.0
+    e = int(math.log(abs(x)) / math.log(2.0)) - 2
+    unit = 2.0 ** (e - bits + 2)
+    while abs(x) / unit >= 2.0 ** bits:
+        unit = unit * 2.0
+    return round(x / unit) * unit
+
+
+def tile_mlaattention_pa_l_kernel(tc, hidden_states, Wqa, Wqb, out):
+    nc = tc.nc
+    x2d = hidden_states.flatten_outer_dims()
+
+    with ExitStack() as ctx:
+        sb = ctx.enter_context(tc.tile_pool(name="sb", bufs=1))
+        ps = ctx.enter_context(tc.psum_pool(name="ps", bufs=1))
+        ctx.enter_context(tc.manual_schedule())
+
+        def sbuf(shape, dtype, tag, kib):
+            return sb.tile(shape, dtype, name=tag, tag=tag, offset=int(kib * KIB), align_bytes=64)
+
+        def bank(i):
+            return ps.tile([P, 512], F32, name="bank%d" % i, tag="bank%d" % i)
+
+        rotation = [0]
+
+        def next_bank():
+            i = rotation[0] % 8
+            rotation[0] = rotation[0] + 1
+            return bank(i)
+
+        def copy_on(engine, dst, src):
+            if engine == "V":
+                nc.vector.tensor_copy(out=dst, in_=src)
+            else:
+                nc.scalar.copy(out=dst, in_=src)
+
+        xraw, xbanks, xgrp, xc, xpl = {}, {}, {}, {}, {}
+
+        def load_x(k):
+            n, cp = divmod(k, 4)
+            xraw[k] = sbuf([P, 4, 1024], BF16, "xraw%d" % (k % 3), XRAW + 8 * (k % 3))
+            nc.sync.dma_start(
+                out=xraw[k][:],
+                in_=x2d[512 * n : 512 * (n + 1), 1024 * cp : 1024 * (cp + 1)].rearrange("(a p) k -> p a k", p=P),
+            )
+
+        def transpose_run(k):
+            words = xraw[k][:].bitcast(F32)
+            for cl in range(2):
+                for hb in range(2):
+                    bk = bank(2 * cl + hb)
+                    xbanks[(k, cl, hb)] = bk
+                    view = bk[:].rearrange("p (a u r) -> p a u r", a=2, u=2)
+                    for a in range(2):
+                        for u in range(2):
+                            nc.tensor.transpose(
+                                view[:, a, u, :],
+                                words[:, 2 * hb + a, 256 * cl + u : 256 * (cl + 1) : 2],
+                                ident[:],
+                            )
+
+        def x_copy(k):
+            for cl in range(2):
+                e = 2 * k + cl
+                xgrp[e] = sbuf([P, 2048], BF16, "xgrp%d" % (e % 3), XGRP + 4 * (e % 3))
+                dst = xgrp[e][:].bitcast(F32).rearrange("p (a r u) -> p a r u", a=4, u=2)
+                for hb in range(2):
+                    src = xbanks[(k, cl, hb)][:].rearrange("p (a u r) -> p a r u", a=2, u=2)
+                    copy_on("V" if hb == 0 else "S", dst[:, 2 * hb : 2 * hb + 2], src)
+
+        def x_quant(k):
+            n, cp = divmod(k, 4)
+            if cp == 0:
+                xc[n] = sbuf([P, 8, 512], U32, "xc%d" % n, XC + 16 * n)
+            for cl in range(2):
+                c = 2 * cp + cl
+                if c % 4 == 0:
+                    xpl[(n, c // 4)] = sbuf([P, 512], U8, "xpl%d_%d" % (n, c // 4), XPL + n + 0.5 * (c // 4))
+                nc.vector.quantize_mx(
+                    out=xc[n][:, c, :].bitcast(FP8X4),
+                    scales=xpl[(n, c // 4)][4 * (c % 4) : P, :],
+                    in_=xgrp[2 * k + cl][:],
+                )
+
+        wraw, wgrp, wc, wpl = {}, {}, {}, {}
+
+        def load_w(g, c):
+            if g == 0 and c % 5 < 3:
+                wraw[(g, c)] = sbuf([P, 4, 512], BF16, "wrawh%d" % (c % 5), WRAWH + 4 * (c % 5))
+            else:
+                s = (c % 5 - 3) if g == 0 else c % 2
+                wraw[(g, c)] = sbuf([P, 4, 512], BF16, "wraw%d" % s, WRAW + 4 * s)
+            nc.sync.dma_start(
+                out=wraw[(g, c)][:],
+                in_=Wqa[512 * c : 512 * (c + 1), 512 * g : 512 * (g + 1)].rearrange("(p j) w -> p j w", j=4),
+            )
+
+        def w_interleave(engine, g, c):
+            wgrp[(g, c)] = sbuf([P, 2048], BF16, "wgrp%d" % (c % 2), WGRP + 4 * (c % 2))
+            copy_on(
+                engine,
+                wgrp[(g, c)][:].rearrange("p (t m j) -> p t m j", t=4, j=4),
+                wraw[(g, c)][:].rearrange("p j (m t) -> p t m j", t=4),
+            )
+
+        def w_scale(g, c, lo, hi):
+            if g == 0:
+                return wpl[0][:, c, lo:hi]
+            return wpl[g][4 * (c % 4) : P, c // 4, lo:hi]
+
+        def w_quant(g, c):
+            if c == 0:
+                wc[g] = sbuf([P, 8, 512], U32, "wc%d" % (g % 2), WCA if g % 2 == 0 else WCB)
+                if g == 0:
+                    wpl[0] = sbuf([P, 8, 512], U8, "wpl_first", WPL0)
+                else:
+                    wpl[g] = sbuf([P, 2, 512], U8, "wpl%d" % (g % 2), WPLA if g % 2 == 0 else WPLB)
+            nc.vector.quantize_mx(out=wc[g][:, c, :].bitcast(FP8X4), scales=w_scale(g, c, 0, 512), in_=wgrp[(g, c)][:])
+
+        def mx_first(acc, g, n, t, c):
+            nc.tensor.matmul_mx(
+                out=acc[:],
+                lhsT=wc[g][:, c, 128 * t : 128 * (t + 1)].bitcast(FP8X4),
+                lhsT_scale=w_scale(g, c, 128 * t, 128 * (t + 1)),
+                rhs=xc[n][:, c, :].bitcast(FP8X4),
+                rhs_scale=xpl[(n, c // 4)][4 * (c % 4) : P, :],
+                start=(c == 0),
+                stop=(c == 7),
+            )
+
+        qst, qgrp, qlc = {}, {}, {}
+        qlpl = sbuf([P, 2, TOKENS], U8, "qlpl", QLPL)
+
+        def ql_evac(engine, e, t, acc):
+            if t == 0:
+                qst[e] = sbuf([P, 4, 512], BF16, "qst%d" % (e % 2), QST + 4 * (e % 2))
+            copy_on(engine, qst[e][:, t, :], acc[:])
+
+        def ql_interleave(e):
+            qgrp[e] = sbuf([P, 2048], BF16, "qgrp", QGRP)
+            nc.vector.tensor_copy(
+                out=qgrp[e][:].rearrange("p (n t) -> p n t", t=4), in_=qst[e][:].rearrange("p t n -> p n t")
+            )
+
+        def ql_codes(g, n):
+            if g < 5:
+                return qlc[g][:, 512 * n : 512 * (n + 1)]
+            return qlc[(5, n)][:]
+
+        def ql_quant(e):
+            g, n = divmod(e, 6)
+            if g < 5 and n == 0:
+                qlc[g] = sbuf([P, TOKENS], U32, "qlc%d" % g, QLC + 12 * g)
+            if g == 5:
+                qlc[(5, n)] = sbuf([P, 512], U32, "qlc5_%d" % n, XC + 16 * n)
+            nc.vector.quantize_mx(
+                out=ql_codes(g, n).bitcast(FP8X4),
+                scales=qlpl[4 * (g % 4) : P, g // 4, 512 * n : 512 * (n + 1)],
+                in_=qgrp[e][:],
+            )
+
+        braw, rgrp, ngrp, bc, bpl = {}, {}, {}, {}, {}
+
+        def load_b(U):
+            sc, u = divmod(U, 12)
+            g2, hf = divmod(u, 2)
+            braw[U] = sbuf([P, 4, 768], BF16, "braw%d" % (U % 3), BRAW + 6 * (U % 3))
+            col = 1536 * sc + 768 * hf
+            nc.sync.dma_start(
+                out=braw[U][:],
+                in_=Wqb[512 * g2 : 512 * (g2 + 1), col : col + 768].rearrange("(p j) w -> p j w", j=4),
+            )
+
+        def b_copy(U, engine_r, engine_n):
+            rgrp[U] = sbuf([P, 2048], BF16, "rgrp%d" % (U % 2), RGRP + 4 * (U % 2))
+            ngrp[U] = sbuf([P, 1024], BF16, "ngrp%d" % (U % 2), NGRP + 2 * (U % 2))
+            src = braw[U][:].rearrange("p j (h d) -> p h d j", d=HEAD)
+            copy_on(engine_r, rgrp[U][:].rearrange("p (h r j) -> p h r j", h=4, j=4), src[:, :, NOPE:HEAD, :])
+            copy_on(engine_n, ngrp[U][:].rearrange("p (h r j) -> p h r j", h=4, j=4), src[:, :, 0:NOPE, :])
+            if U + 3 < 24:
+                load_b(U + 3)
+
+        def cell(sc, i):
+            return XC + 16 * (3 * sc + i // 7) + 2 + 2 * (i % 7)
+
+        def b_quant(U):
+            sc, u = divmod(U, 12)
+            g2, hf = divmod(u, 2)
+            if u == 0:
+                for bk in range(3):
+                    bpl[(sc, bk)] = sbuf([P, 2, 512], U8, "bpl%d_%d" % (sc, bk), (BPL0 if sc == 0 else BPL1) + bk)
+            bc[(sc, hf, g2)] = sbuf([P, 512], U32, "bc%d_%d_%d" % (sc, hf, g2), cell(sc, 3 * g2 + 2 * hf))
+            if hf == 0:
+                bc[(sc, 2, g2)] = sbuf([P, 512], U32, "bc%d_2_%d" % (sc, g2), cell(sc, 3 * g2 + 1))
+            k = 4 * (g2 % 4)
+            nc.vector.quantize_mx(
+                out=bc[(sc, hf, g2)][:].bitcast(FP8X4), scales=bpl[(sc, hf)][k:P, g2 // 4, :], in_=rgrp[U][:]
+            )
+            nc.vector.quantize_mx(
+                out=bc[(sc, 2, g2)][:, 256 * hf : 256 * (hf + 1)].bitcast(FP8X4),
+                scales=bpl[(sc, 2)][k:P, g2 // 4, 256 * hf : 256 * (hf + 1)],
+                in_=ngrp[U][:],
+            )
+
+        tabs = {}
+
+        def table_constants():
+            frq = sbuf([P, 3, 64], F32, "frq", FRQ)
+            tabs["frq"] = frq
+            for i in range(64):
+                turns = 10000.0 ** (-2.0 * i / 128.0) / (2.0 * PI)
+                a = round_bits(turns, 12)
+                b = round_bits(turns - a, 12)
+                c = round_bits(turns - a - b, 24)
+                nc.gpsimd.memset(frq[:, 0, i : i + 1], a)
+                nc.gpsimd.memset(frq[:, 1, i : i + 1], b)
+                nc.gpsimd.memset(frq[:, 2, i : i + 1], c)
+            tabs["pos"] = sbuf([P, 12, 64], F32, "tmp0", TMP)
+            nc.gpsimd.iota(
+                tabs["pos"][:], pattern=[[128, 12], [0, 64]], base=0, channel_multiplier=1,
+                allow_small_or_imprecise_dtypes=True,
+            )
+
+        def tmp(j, dtype):
+            return sbuf([P, 12, 64], dtype, "tmp%d" % j, TMP + 3 * j)
+
+        def part(j):
+            return tabs["frq"][:, j, :].unsqueeze(1).to_broadcast([P, 12, 64])
+
+        def wrap(dst, src):
+            nc.vector.scalar_tensor_tensor(out=dst[:], in0=src[:], scalar=0.5, in1=src[:], op0=ALU.is_gt, op1=ALU.subtract)
+
+        def table_step(s):
+            t = tabs
+            if s == 0:
+                t["u"] = tmp(1, F32)
+                nc.vector.tensor_tensor(out=t["u"][:], in0=t["pos"][:], in1=part(0), op=ALU.mult)
+            elif s == 1:
+                t["ki"] = tmp(2, I32)
+                nc.vector.tensor_copy(out=t["ki"][:], in_=t["u"][:])
+            elif s == 2:
+                t["kf"] = tmp(3, F32)
+                nc.vector.tensor_copy(out=t["kf"][:], in_=t["ki"][:])
+            elif s == 3:
+                t["f"] = tmp(4, F32)
+                nc.vector.tensor_tensor(out=t["f"][:], in0=t["u"][:], in1=t["kf"][:], op=ALU.subtract)
+            elif s == 4:
+                t["v"] = tmp(5, F32)
+                nc.vector.tensor_tensor(out=t["v"][:], in0=t["pos"][:], in1=part(1), op=ALU.mult)
+            elif s == 5:
+                t["f2"] = tmp(6, F32)
+                nc.vector.tensor_tensor(out=t["f2"][:], in0=t["f"][:], in1=t["v"][:], op=ALU.add)
+            elif s == 6:
+                t["v2"] = tmp(1, F32)
+                nc.vector.tensor_tensor(out=t["v2"][:], in0=t["pos"][:], in1=part(2), op=ALU.mult)
+            elif s == 7:
+                t["f3"] = tmp(2, F32)
+                nc.vector.tensor_tensor(out=t["f3"][:], in0=t["f2"][:], in1=t["v2"][:], op=ALU.add)
+            elif s == 8:
+                t["g1"] = tmp(3, F32)
+                wrap(t["g1"], t["f3"])
+            elif s == 9:
+                t["fw"] = tmp(4, F32)
+                wrap(t["fw"], t["g1"])
+            elif s == 10:
+                t["sin"] = sbuf([P, 12, 64], F32, "sin", TAB + 3)
+                nc.scalar.activation(out=t["sin"][:], in_=t["fw"][:], func=ACT.Sin, scale=2.0 * PI)
+                t["fc"] = tmp(5, F32)
+                nc.vector.tensor_scalar_add(out=t["fc"][:], in0=t["fw"][:], scalar1=0.25)
+            elif s == 11:
+                t["gc"] = tmp(6, F32)
+                wrap(t["gc"], t["fc"])
+            elif s == 12:
+                t["cos"] = sbuf([P, 12, 64], F32, "cos", TAB)
+                nc.scalar.activation(out=t["cos"][:], in_=t["gc"][:], func=ACT.Sin, scale=-2.0 * PI)
+
+        ident = sbuf([P, P], F32, "ident", IDENT)
+        make_identity(nc, ident[:])
+
+        load_x(0)
+        load_x(1)
+        load_w(0, 0)
+        load_w(0, 1)
+        load_x(2)
+        load_w(0, 2)
+        load_w(0, 3)
+        load_w(0, 4)
+
+        acc = {}
+        for k in range(26):
+            if k < 24:
+                transpose_run(k)
+                if k + 3 < 24:
+                    load_x(k + 3)
+                x_copy(k)
+                x_quant(k)
+            if k >= 2:
+                n, cp = divmod(k - 2, 4)
+                if cp == 0:
+                    for t in range(4):
+                        acc[t] = bank(4 + t)
+                for c in (2 * cp, 2 * cp + 1):
+                    for t in range(4):
+                        mx_first(acc[t], 0, n, t, c)
+                if cp == 3:
+                    for t in range(4):
+                        ql_evac("S" if t % 2 == 0 else "V", n, t, acc[t])
+            if 1 <= k <= 4:
+                a = 2 * (k - 1)
+                w_interleave("S", 0, a)
+                w_interleave("V", 0, a + 1)
+                w_quant(0, a)
+                w_quant(0, a + 1)
+                if a + 5 < 8:
+                    load_w(0, a + 5)
+                if a + 6 < 8:
+                    load_w(0, a + 6)
+                if k == 4:
+                    load_w(1, 0)
+                    load_w(1, 1)
+            if k >= 6 and k % 2 == 0 and k <= 20:
+                c = (k - 6) // 2
+                w_interleave("S", 1, c)
+                if c + 2 < 8:
+                    load_w(1, c + 2)
+                else:
+                    load_w(2, c - 6)
+            if k >= 7 and k % 2 == 1 and k <= 21:
+                w_quant(1, (k - 7) // 2)
+            if k >= 6 and k % 4 == 2:
+                ql_interleave((k - 6) // 4)
+            if k >= 7 and k % 4 == 3:
+                ql_quant((k - 7) // 4)
+
+        table_constants()
+
+        for g in range(1, 6):
+            for n in range(6):
+                e = 6 * g + n
+                for t in range(4):
+                    pos = 4 * n + t
+                    a = next_bank()
+                    for c in range(8):
+                        mx_first(a, g, n, t, c)
+                    ql_evac("S", e, t, a)
+                    if g < 5 and pos < 16:
+                        c = pos // 2
+                        if pos % 2 == 0:
+                            w_interleave("S" if c % 2 == 0 else "V", g + 1, c)
+                            if c + 2 < 8:
+                                load_w(g + 1, c + 2)
+                            elif g + 2 < 6:
+                                load_w(g + 2, c - 6)
+                        else:
+                            w_quant(g + 1, c)
+                    if g == 5:
+                        if pos == 0:
+                            load_b(0)
+                            load_b(1)
+                            load_b(2)
+                        for u in range(12):
+                            if pos == 4 + (3 * u) // 2:
+                                b_copy(u, "S" if u % 2 == 0 else "V", "V")
+                        for u in range(12):
+                            if pos == 5 + (3 * u) // 2:
+                                b_quant(u)
+                    if t == 1:
+                        ql_interleave(e - 1)
+                    if t == 2:
+                        ql_quant(e - 1)
+                    if g == 2 and pos < 13:
+                        table_step(pos)
+        ql_interleave(35)
+        ql_quant(35)
+
+        outt, ra, rb = {}, {}, {}
+        pending = []
+
+        def rope_head(s, bk, a):
+            x = 2 * s + bk
+            pt = (s % 24) % 12
+            xv = a[:].rearrange("p (h i two) -> p h two i", h=4, two=2)
+            rb[x] = sbuf([P, 4, 2, 64], F32, "rb%d" % (x % 2), RTMP + 4 * (x % 2) + 2)
+            sin3 = tabs["sin"][:, pt, :].unsqueeze(1).to_broadcast([P, 4, 64])
+            nc.vector.scalar_tensor_tensor(
+                out=rb[x][:, :, 0, :], in0=xv[:, :, 1, :], scalar=-1.0, in1=sin3, op0=ALU.mult, op1=ALU.mult
+            )
+            nc.vector.tensor_tensor(out=rb[x][:, :, 1, :], in0=xv[:, :, 0, :], in1=sin3, op=ALU.mult)
+            rope_tail()
+            ra[x] = sbuf([P, 4, 2, 64], F32, "ra%d" % (x % 2), RTMP + 4 * (x % 2))
+            cos4 = tabs["cos"][:, pt, :].unsqueeze(1).unsqueeze(1).to_broadcast([P, 4, 2, 64])
+            nc.vector.tensor_tensor(out=ra[x][:], in0=xv, in1=cos4, op=ALU.mult)
+            pending.append((s, bk))
+
+        def rope_tail():
+            if len(pending) == 0:
+                return
+            s, bk = pending.pop(0)
+            x = 2 * s + bk
+            nc.vector.tensor_tensor(
+                out=outt[s][:, 4 * bk : 4 * bk + 4, NOPE:HEAD].rearrange("p h (i two) -> p h i two", two=2),
+                in0=ra[x][:].rearrange("p h two i -> p h i two"),
+                in1=rb[x][:].rearrange("p h two i -> p h i two"),
+                op=ALU.add,
+            )
+            if bk == 1:
+                sc, tt = divmod(s, 24)
+                b, p0 = divmod(128 * tt, SEQ)
+                nc.scalar.dma_start(
+                    out=out[b, 8 * sc : 8 * sc + 8, p0 : p0 + P, :].rearrange("h p d -> p h d"), in_=outt[s][:]
+                )
+
+        for s in range(48):
+            sc, tt = divmod(s, 24)
+            outt[s] = sbuf([P, 8, HEAD], F32, "outt%d" % (s % 3), OUTT + 6 * (s % 3))
+            for bk in range(3):
+                a = next_bank()
+                for g2 in range(6):
+                    k = 4 * (g2 % 4)
+                    nc.tensor.matmul_mx(
+                        out=a[:],
+                        lhsT=ql_codes(g2, tt // 4)[:, 128 * (tt % 4) : 128 * (tt % 4 + 1)].bitcast(FP8X4),
+                        lhsT_scale=qlpl[k:P, g2 // 4, 128 * tt : 128 * (tt + 1)],
+                        rhs=bc[(sc, bk, g2)][:].bitcast(FP8X4),
+                        rhs_scale=bpl[(sc, bk)][k:P, g2 // 4, :],
+                        start=(g2 == 0),
+                        stop=(g2 == 5),
+                    )
+                if bk < 2:
+                    rope_head(s, bk, a)
+                else:
+                    nc.scalar.copy(out=outt[s][:, :, 0:NOPE], in_=a[:].rearrange("p (h r) -> p h r", h=8))
+                if bk == 1 and sc == 0:
+                    if tt % 2 == 0:
+                        b_copy(12 + tt // 2, "S", "S")
+                    else:
+                        b_quant(12 + tt // 2)
+        rope_tail()
+        rope_tail()

@@ -25,6 +25,7 @@ FLOPS = 2 * TOKENS * D_IN * LATENT + 2 * TOKENS * LATENT * HEADS * HEAD
 
 KIB = 1024
 PI = 3.141592653589793
+FIRST_SORTED = 6
 QLC = 0
 QLPL = 60
 XC = 66
@@ -39,8 +40,9 @@ QGRP = 218
 QST = 222
 TAB = 230
 WRAWH = 12
-XRAW = 24
-XGRP = 48
+XSORT = 12
+XRAW = 28
+XGRP = 52
 IDENT = 230
 WPL0 = 231
 FRQ = 36
@@ -92,7 +94,7 @@ def tile_mlaattention_pa_l_kernel(tc, hidden_states, Wqa, Wqb, out):
             else:
                 nc.scalar.copy(out=dst, in_=src)
 
-        xraw, xbanks, xgrp, xc, xpl = {}, {}, {}, {}, {}
+        xraw, xsort, xbanks, xgrp, xc, xpl = {}, {}, {}, {}, {}, {}
 
         def load_x(k):
             n, cp = divmod(k, 4)
@@ -101,6 +103,15 @@ def tile_mlaattention_pa_l_kernel(tc, hidden_states, Wqa, Wqb, out):
                 out=xraw[k][:],
                 in_=x2d[512 * n : 512 * (n + 1), 1024 * cp : 1024 * (cp + 1)].rearrange("(a p) k -> p a k", p=P),
             )
+
+        def x_sort(k):
+            xsort[k] = sbuf([P, 8, 2, 128], F32, "xsort%d" % (k % 2), XSORT + 8 * (k % 2))
+            nc.vector.tensor_copy(
+                out=xsort[k][:],
+                in_=xraw[k][:].bitcast(F32).rearrange("p a w -> p (a w)").rearrange("p (b m u) -> p b u m", b=8, u=2),
+            )
+            if k + 3 < 24:
+                load_x(k + 3)
 
         def transpose_run(k):
             words = xraw[k][:].bitcast(F32)
@@ -111,20 +122,20 @@ def tile_mlaattention_pa_l_kernel(tc, hidden_states, Wqa, Wqb, out):
                     view = bk[:].rearrange("p (a u r) -> p a u r", a=2, u=2)
                     for a in range(2):
                         for u in range(2):
-                            nc.tensor.transpose(
-                                view[:, a, u, :],
-                                words[:, 2 * hb + a, 256 * cl + u : 256 * (cl + 1) : 2],
-                                ident[:],
-                            )
+                            if k >= FIRST_SORTED:
+                                src = xsort[k][:, 2 * (2 * hb + a) + cl, u, :]
+                            else:
+                                src = words[:, 2 * hb + a, 256 * cl + u : 256 * (cl + 1) : 2]
+                            nc.tensor.transpose(view[:, a, u, :], src, ident[:])
 
         def x_copy(k):
             for cl in range(2):
                 e = 2 * k + cl
-                xgrp[e] = sbuf([P, 2048], BF16, "xgrp%d" % (e % 3), XGRP + 4 * (e % 3))
+                xgrp[e] = sbuf([P, 2048], BF16, "xgrp%d" % (e % 2), XGRP + 4 * (e % 2))
                 dst = xgrp[e][:].bitcast(F32).rearrange("p (a r u) -> p a r u", a=4, u=2)
                 for hb in range(2):
                     src = xbanks[(k, cl, hb)][:].rearrange("p (a u r) -> p a r u", a=2, u=2)
-                    copy_on("V" if hb == 0 else "S", dst[:, 2 * hb : 2 * hb + 2], src)
+                    copy_on("V" if (k % 4 == 1 and cl == 0 and hb == 1) else "S", dst[:, 2 * hb : 2 * hb + 2], src)
 
         def x_quant(k):
             n, cp = divmod(k, 4)
@@ -342,14 +353,17 @@ def tile_mlaattention_pa_l_kernel(tc, hidden_states, Wqa, Wqb, out):
         load_x(2)
         load_w(0, 2)
         load_w(0, 3)
-        load_w(0, 4)
 
         acc = {}
         for k in range(26):
+            if FIRST_SORTED <= k + 1 < 24:
+                x_sort(k + 1)
             if k < 24:
                 transpose_run(k)
-                if k + 3 < 24:
+                if k + 3 < 24 and k < FIRST_SORTED:
                     load_x(k + 3)
+                if k == 0:
+                    load_w(0, 4)
                 x_copy(k)
                 x_quant(k)
             if k >= 2:

@@ -168,8 +168,8 @@ def tile_mlaattention_pa_l_kernel(tc, hidden_states, Wqa, Wqb, out):
             wgrp[(g, c)] = sbuf([P, 2048], BF16, "wgrp%d" % (c % 2), WGRP + 4 * (c % 2))
             copy_on(
                 engine,
-                wgrp[(g, c)][:].rearrange("p (t m j) -> p t m j", t=4, j=4),
-                wraw[(g, c)][:].rearrange("p j (m t) -> p t m j", t=4),
+                wgrp[(g, c)][:].rearrange("p (t m j) -> p m j t", t=4, j=4),
+                wraw[(g, c)][:].rearrange("p j (m t) -> p m j t", t=4),
             )
 
         def w_scale(g, c, lo, hi):
@@ -208,7 +208,8 @@ def tile_mlaattention_pa_l_kernel(tc, hidden_states, Wqa, Wqb, out):
         def ql_interleave(e):
             qgrp[e] = sbuf([P, 2048], BF16, "qgrp", QGRP)
             nc.vector.tensor_copy(
-                out=qgrp[e][:].rearrange("p (n t) -> p n t", t=4), in_=qst[e][:].rearrange("p t n -> p n t")
+                out=qgrp[e][:].rearrange("p (c i t) -> p c t i", i=4, t=4),
+                in_=qst[e][:].rearrange("p t (c i) -> p c t i", i=4),
             )
 
         def ql_codes(g, n):

@@ -164,12 +164,13 @@ def tile_mlaattention_pa_l_kernel(tc, hidden_states, Wqa, Wqb, out):
                 in_=Wqa[512 * c : 512 * (c + 1), 512 * g : 512 * (g + 1)].rearrange("(p j) w -> p j w", j=4),
             )
 
-        def w_interleave(engine, g, c):
-            wgrp[(g, c)] = sbuf([P, 2048], BF16, "wgrp%d" % (c % 2), WGRP + 4 * (c % 2))
+        def w_interleave(engine, g, c, lo=0, hi=128):
+            if lo == 0:
+                wgrp[(g, c)] = sbuf([P, 2048], BF16, "wgrp%d" % (c % 2), WGRP + 4 * (c % 2))
             copy_on(
                 engine,
-                wgrp[(g, c)][:].rearrange("p (t m j) -> p m j t", t=4, j=4),
-                wraw[(g, c)][:].rearrange("p j (m t) -> p m j t", t=4),
+                wgrp[(g, c)][:].rearrange("p (t m j) -> p m j t", t=4, j=4)[:, lo:hi],
+                wraw[(g, c)][:].rearrange("p j (m t) -> p m j t", t=4)[:, lo:hi],
             )
 
         def w_scale(g, c, lo, hi):
@@ -202,7 +203,13 @@ def tile_mlaattention_pa_l_kernel(tc, hidden_states, Wqa, Wqb, out):
 
         def ql_evac(engine, e, t, acc):
             if t == 0:
-                qst[e] = sbuf([P, 4, 512], BF16, "qst%d" % (e % 2), QST + 4 * (e % 2))
+                if e < 3:
+                    qst[e] = sbuf([P, 4, 512], BF16, "qhold%d" % e, QLC + 4 * e)
+                elif e == 5:
+                    qst[e] = sbuf([P, 4, 512], BF16, "qhold5", XGRP)
+                else:
+                    s = (e + 1) % 2 if e < 5 else e % 2
+                    qst[e] = sbuf([P, 4, 512], BF16, "qst%d" % s, QST + 4 * s)
             copy_on(engine, qst[e][:, t, :], acc[:])
 
         def ql_interleave(e):
@@ -213,14 +220,16 @@ def tile_mlaattention_pa_l_kernel(tc, hidden_states, Wqa, Wqb, out):
             )
 
         def ql_codes(g, n):
-            if g < 5:
+            if 0 < g < 5:
                 return qlc[g][:, 512 * n : 512 * (n + 1)]
-            return qlc[(5, n)][:]
+            return qlc[(g, n)][:]
 
         def ql_quant(e):
             g, n = divmod(e, 6)
-            if g < 5 and n == 0:
+            if 0 < g < 5 and n == 0:
                 qlc[g] = sbuf([P, TOKENS], U32, "qlc%d" % g, QLC + 12 * g)
+            if g == 0:
+                qlc[(0, n)] = sbuf([P, 512], U32, "qlc0_%d" % n, QLC + 2 * n)
             if g == 5:
                 qlc[(5, n)] = sbuf([P, 512], U32, "qlc5_%d" % n, XC + 16 * n)
             nc.vector.quantize_mx(
@@ -391,27 +400,56 @@ def tile_mlaattention_pa_l_kernel(tc, hidden_states, Wqa, Wqb, out):
                 if k == 4:
                     load_w(1, 0)
                     load_w(1, 1)
-            if k >= 6 and k % 2 == 0 and k <= 20:
-                c = (k - 6) // 2
-                w_interleave("S", 1, c)
-                if c + 2 < 8:
+            if 6 <= k < 22:
+                c, step = divmod(k - 6, 4)
+                if step == 0:
+                    w_interleave("S", 1, c, 0, 64)
+                if step == 1:
+                    w_interleave("S", 1, c, 64, 128)
                     load_w(1, c + 2)
-                else:
-                    load_w(2, c - 6)
-            if k >= 7 and k % 2 == 1 and k <= 21:
-                w_quant(1, (k - 7) // 2)
-            if k >= 6 and k % 4 == 2:
-                ql_interleave((k - 6) // 4)
-            if k >= 7 and k % 4 == 3:
-                ql_quant((k - 7) // 4)
+                if step == 2:
+                    w_quant(1, c)
+            if k == 24:
+                w_interleave("S", 1, 4)
+                w_interleave("V", 1, 5)
+                load_w(1, 6)
+                load_w(1, 7)
+            if k == 25:
+                w_quant(1, 4)
+                w_quant(1, 5)
 
         table_constants()
 
+        pair = {}
+        for n in range(2):
+            for t in range(4):
+                pair[(n, t)] = next_bank()
+        for c in range(8):
+            if c == 0:
+                w_interleave("S", 1, 6)
+                w_interleave("V", 1, 7)
+                load_w(2, 0)
+                load_w(2, 1)
+            for n in range(2):
+                for t in range(4):
+                    mx_first(pair[(n, t)], 1, n, t, c)
+            if c == 1:
+                w_quant(1, 6)
+                w_quant(1, 7)
+            if 1 <= c < 7:
+                ql_quant(c - 1)
+            if c < 6:
+                ql_interleave(c)
+        for n in range(2):
+            for t in range(4):
+                ql_evac("S" if t % 2 == 0 else "V", 6 + n, t, pair[(n, t)])
+        ql_interleave(6)
+
         for g in range(1, 6):
-            for n in range(6):
+            for n in range(2 if g == 1 else 0, 6):
                 e = 6 * g + n
                 for t in range(4):
-                    pos = 4 * n + t
+                    pos = 4 * n + t - (8 if g == 1 else 0)
                     a = next_bank()
                     for c in range(8):
                         mx_first(a, g, n, t, c)
@@ -437,6 +475,8 @@ def tile_mlaattention_pa_l_kernel(tc, hidden_states, Wqa, Wqb, out):
                         for u in range(12):
                             if pos == 5 + (3 * u) // 2:
                                 b_quant(u)
+                    if e == 8 and t == 0:
+                        ql_quant(6)
                     if t == 1:
                         ql_interleave(e - 1)
                     if t == 2:
@@ -504,9 +544,11 @@ def tile_mlaattention_pa_l_kernel(tc, hidden_states, Wqa, Wqb, out):
                 else:
                     nc.scalar.copy(out=outt[s][:, :, 0:NOPE], in_=a[:].rearrange("p (h r) -> p h r", h=8))
                 if bk == 1 and sc == 0:
-                    if tt % 2 == 0:
-                        b_copy(12 + tt // 2, "S", "S")
-                    else:
-                        b_quant(12 + tt // 2)
+                    for u in range(12):
+                        if tt == (5 * u) // 3:
+                            b_copy(12 + u, "S", "S")
+                    for u in range(12):
+                        if tt == (5 * u) // 3 + 1:
+                            b_quant(12 + u)
         rope_tail()
         rope_tail()

from contextlib import ExitStack
import math

import concourse.mybir as mybir
from concourse.masks import make_identity

F32 = mybir.dt.float32
BF16 = mybir.dt.bfloat16
U32 = mybir.dt.uint32
U8 = mybir.dt.uint8
I32 = mybir.dt.int32
FP8X4 = mybir.dt.float8_e4m3fn_x4
ALU = mybir.AluOpType
ACT = mybir.ActivationFunctionType

P = 128
TOKENS = 3072
SEQ = 1536
D_IN = 4096
LATENT = 3072
HEADS = 16
HEAD = 192
NOPE = 64
FLOPS = 2 * TOKENS * D_IN * LATENT + 2 * TOKENS * LATENT * HEADS * HEAD

KIB = 1024
PI = 3.141592653589793
FIRST_SORTED = 6
QLC = 0
QLPL = 60
XC = 66
XPL = 162
WCB = 168
WPLB = 184
WCA = 185
WPLA = 201
WRAW = 202
WGRP = 210
QGRP = 218
QST = 222
TAB = 230
WRAWH = 12
XSORT = 12
XRAW = 28
XGRP = 52
IDENT = 230
WPL0 = 231
FRQ = 36
TMP = 37
BRAW = 185
RGRP = 203
NGRP = 211
BPL0 = 215
OUTT = 156
BPL1 = 174
RTMP = 177


def round_bits(x, bits):
    if x == 0.0:
        return 0.0
    e = int(math.log(abs(x)) / math.log(2.0)) - 2
    unit = 2.0 ** (e - bits + 2)
    while abs(x) / unit >= 2.0 ** bits:
        unit = unit * 2.0
    return round(x / unit) * unit


def tile_mlaattention_pa_l_kernel(tc, hidden_states, Wqa, Wqb, out):
    nc = tc.nc
    x2d = hidden_states.flatten_outer_dims()

    with ExitStack() as ctx:
        sb = ctx.enter_context(tc.tile_pool(name="sb", bufs=1))
        ps = ctx.enter_context(tc.psum_pool(name="ps", bufs=1))
        ctx.enter_context(tc.manual_schedule())

        def sbuf(shape, dtype, tag, kib):
            return sb.tile(shape, dtype, name=tag, tag=tag, offset=int(kib * KIB), align_bytes=64)

        def bank(i):
            return ps.tile([P, 512], F32, name="bank%d" % i, tag="bank%d" % i)

        rotation = [0]

        def next_bank():
            i = rotation[0] % 8
            rotation[0] = rotation[0] + 1
            return bank(i)

        def copy_on(engine, dst, src):
            if engine == "V":
                nc.vector.tensor_copy(out=dst, in_=src)
            else:
                nc.scalar.copy(out=dst, in_=src)

        xraw, xsort, xbanks, xgrp, xc, xpl = {}, {}, {}, {}, {}, {}

        def load_x(k):
            n, cp = divmod(k, 4)
            xraw[k] = sbuf([P, 4, 1024], BF16, "xraw%d" % (k % 3), XRAW + 8 * (k % 3))
            nc.sync.dma_start(
                out=xraw[k][:],
                in_=x2d[512 * n : 512 * (n + 1), 1024 * cp : 1024 * (cp + 1)].rearrange("(a p) k -> p a k", p=P),
            )

        def x_sort(k):
            xsort[k] = sbuf([P, 8, 2, 128], F32, "xsort%d" % (k % 2), XSORT + 8 * (k % 2))
            nc.vector.tensor_copy(
                out=xsort[k][:],
                in_=xraw[k][:].bitcast(F32).rearrange("p a w -> p (a w)").rearrange("p (b m u) -> p b u m", b=8, u=2),
            )
            if k + 3 < 24:
                load_x(k + 3)

        def transpose_run(k):
            words = xraw[k][:].bitcast(F32)
            for cl in range(2):
                for hb in range(2):
                    bk = bank(2 * cl + hb)
                    xbanks[(k, cl, hb)] = bk
                    view = bk[:].rearrange("p (a u r) -> p a u r", a=2, u=2)
                    for a in range(2):
                        for u in range(2):
                            if k >= FIRST_SORTED:
                                src = xsort[k][:, 2 * (2 * hb + a) + cl, u, :]
                            else:
                                src = words[:, 2 * hb + a, 256 * cl + u : 256 * (cl + 1) : 2]
                            nc.tensor.transpose(view[:, a, u, :], src, ident[:])

        def x_copy(k):
            for cl in range(2):
                e = 2 * k + cl
                xgrp[e] = sbuf([P, 2048], BF16, "xgrp%d" % (e % 2), XGRP + 4 * (e % 2))
                dst = xgrp[e][:].bitcast(F32).rearrange("p (a r u) -> p a r u", a=4, u=2)
                for hb in range(2):
                    src = xbanks[(k, cl, hb)][:].rearrange("p (a u r) -> p a r u", a=2, u=2)
                    copy_on("V" if (k % 4 == 1 and cl == 0 and hb == 1) else "S", dst[:, 2 * hb : 2 * hb + 2], src)

        def x_quant(k):
            n, cp = divmod(k, 4)
            if cp == 0:
                xc[n] = sbuf([P, 8, 512], U32, "xc%d" % n, XC + 16 * n)
            for cl in range(2):
                c = 2 * cp + cl
                if c % 4 == 0:
                    xpl[(n, c // 4)] = sbuf([P, 512], U8, "xpl%d_%d" % (n, c // 4), XPL + n + 0.5 * (c // 4))
                nc.vector.quantize_mx(
                    out=xc[n][:, c, :].bitcast(FP8X4),
                    scales=xpl[(n, c // 4)][4 * (c % 4) : P, :],
                    in_=xgrp[2 * k + cl][:],
                )

        wraw, wgrp, wc, wpl = {}, {}, {}, {}

        def load_w(g, c):
            if g == 0 and c % 5 < 3:
                wraw[(g, c)] = sbuf([P, 4, 512], BF16, "wrawh%d" % (c % 5), WRAWH + 4 * (c % 5))
            else:
                s = (c % 5 - 3) if g == 0 else c % 2
                wraw[(g, c)] = sbuf([P, 4, 512], BF16, "wraw%d" % s, WRAW + 4 * s)
            nc.sync.dma_start(
                out=wraw[(g, c)][:],
                in_=Wqa[512 * c : 512 * (c + 1), 512 * g : 512 * (g + 1)].rearrange("(p j) w -> p j w", j=4),
            )

        def w_interleave(engine, g, c, lo=0, hi=128):
            if lo == 0:
                wgrp[(g, c)] = sbuf([P, 2048], BF16, "wgrp%d" % (c % 2), WGRP + 4 * (c % 2))
            copy_on(
                engine,
                wgrp[(g, c)][:].rearrange("p (t m j) -> p m j t", t=4, j=4)[:, lo:hi],
                wraw[(g, c)][:].rearrange("p j (m t) -> p m j t", t=4)[:, lo:hi],
            )

        def w_scale(g, c, lo, hi):
            if g == 0:
                return wpl[0][:, c, lo:hi]
            return wpl[g][4 * (c % 4) : P, c // 4, lo:hi]

        def w_quant(g, c):
            if c == 0:
                wc[g] = sbuf([P, 8, 512], U32, "wc%d" % (g % 2), WCA if g % 2 == 0 else WCB)
                if g == 0:
                    wpl[0] = sbuf([P, 8, 512], U8, "wpl_first", WPL0)
                else:
                    wpl[g] = sbuf([P, 2, 512], U8, "wpl%d" % (g % 2), WPLA if g % 2 == 0 else WPLB)
            nc.vector.quantize_mx(out=wc[g][:, c, :].bitcast(FP8X4), scales=w_scale(g, c, 0, 512), in_=wgrp[(g, c)][:])

        def mx_first(acc, g, n, t, c):
            nc.tensor.matmul_mx(
                out=acc[:],
                lhsT=wc[g][:, c, 128 * t : 128 * (t + 1)].bitcast(FP8X4),
                lhsT_scale=w_scale(g, c, 128 * t, 128 * (t + 1)),
                rhs=xc[n][:, c, :].bitcast(FP8X4),
                rhs_scale=xpl[(n, c // 4)][4 * (c % 4) : P, :],
                start=(c == 0),
                stop=(c == 7),
            )

        qst, qgrp, qlc = {}, {}, {}
        qlpl = sbuf([P, 2, TOKENS], U8, "qlpl", QLPL)

        def ql_evac(engine, e, t, acc):
            if t == 0:
                if e < 3:
                    qst[e] = sbuf([P, 4, 512], BF16, "qhold%d" % e, QLC + 4 * e)
                elif e == 5:
                    qst[e] = sbuf([P, 4, 512], BF16, "qhold5", XGRP)
                else:
                    s = (e + 1) % 2 if e < 5 else e % 2
                    qst[e] = sbuf([P, 4, 512], BF16, "qst%d" % s, QST + 4 * s)
            copy_on(engine, qst[e][:, t, :], acc[:])

        def ql_interleave(e):
            qgrp[e] = sbuf([P, 2048], BF16, "qgrp", QGRP)
            nc.vector.tensor_copy(
                out=qgrp[e][:].rearrange("p (c i t) -> p c t i", i=4, t=4),
                in_=qst[e][:].rearrange("p t (c i) -> p c t i", i=4),
            )

        def ql_codes(g, n):
            if 0 < g < 5:
                return qlc[g][:, 512 * n : 512 * (n + 1)]
            return qlc[(g, n)][:]

        def ql_quant(e):
            g, n = divmod(e, 6)
            if 0 < g < 5 and n == 0:
                qlc[g] = sbuf([P, TOKENS], U32, "qlc%d" % g, QLC + 12 * g)
            if g == 0:
                qlc[(0, n)] = sbuf([P, 512], U32, "qlc0_%d" % n, QLC + 2 * n)
            if g == 5:
                qlc[(5, n)] = sbuf([P, 512], U32, "qlc5_%d" % n, XC + 16 * n)
            nc.vector.quantize_mx(
                out=ql_codes(g, n).bitcast(FP8X4),
                scales=qlpl[4 * (g % 4) : P, g // 4, 512 * n : 512 * (n + 1)],
                in_=qgrp[e][:],
            )

        braw, rgrp, ngrp, bc, bpl = {}, {}, {}, {}, {}

        def load_b(U):
            sc, u = divmod(U, 12)
            g2, hf = divmod(u, 2)
            braw[U] = sbuf([P, 4, 768], BF16, "braw%d" % (U % 3), BRAW + 6 * (U % 3))
            col = 1536 * sc + 768 * hf
            nc.sync.dma_start(
                out=braw[U][:],
                in_=Wqb[512 * g2 : 512 * (g2 + 1), col : col + 768].rearrange("(p j) w -> p j w", j=4),
            )

        def b_copy(U, engine_r, engine_n):
            rgrp[U] = sbuf([P, 2048], BF16, "rgrp%d" % (U % 2), RGRP + 4 * (U % 2))
            ngrp[U] = sbuf([P, 1024], BF16, "ngrp%d" % (U % 2), NGRP + 2 * (U % 2))
            src = braw[U][:].rearrange("p j (h d) -> p h d j", d=HEAD)
            copy_on(engine_r, rgrp[U][:].rearrange("p (h r j) -> p h r j", h=4, j=4), src[:, :, NOPE:HEAD, :])
            copy_on(engine_n, ngrp[U][:].rearrange("p (h r j) -> p h r j", h=4, j=4), src[:, :, 0:NOPE, :])
            if U + 3 < 24:
                load_b(U + 3)

        def cell(sc, i):
            return XC + 16 * (3 * sc + i // 7) + 2 + 2 * (i % 7)

        def b_quant(U):
            sc, u = divmod(U, 12)
            g2, hf = divmod(u, 2)
            if u == 0:
                for bk in range(3):
                    bpl[(sc, bk)] = sbuf([P, 2, 512], U8, "bpl%d_%d" % (sc, bk), (BPL0 if sc == 0 else BPL1) + bk)
            bc[(sc, hf, g2)] = sbuf([P, 512], U32, "bc%d_%d_%d" % (sc, hf, g2), cell(sc, 3 * g2 + 2 * hf))
            if hf == 0:
                bc[(sc, 2, g2)] = sbuf([P, 512], U32, "bc%d_2_%d" % (sc, g2), cell(sc, 3 * g2 + 1))
            k = 4 * (g2 % 4)
            nc.vector.quantize_mx(
                out=bc[(sc, hf, g2)][:].bitcast(FP8X4), scales=bpl[(sc, hf)][k:P, g2 // 4, :], in_=rgrp[U][:]
            )
            nc.vector.quantize_mx(
                out=bc[(sc, 2, g2)][:, 256 * hf : 256 * (hf + 1)].bitcast(FP8X4),
                scales=bpl[(sc, 2)][k:P, g2 // 4, 256 * hf : 256 * (hf + 1)],
                in_=ngrp[U][:],
            )

        tabs = {}

        def table_constants():
            frq = sbuf([P, 3, 64], F32, "frq", FRQ)
            tabs["frq"] = frq
            for i in range(64):
                turns = 10000.0 ** (-2.0 * i / 128.0) / (2.0 * PI)
                a = round_bits(turns, 12)
                b = round_bits(turns - a, 12)
                c = round_bits(turns - a - b, 24)
                nc.gpsimd.memset(frq[:, 0, i : i + 1], a)
                nc.gpsimd.memset(frq[:, 1, i : i + 1], b)
                nc.gpsimd.memset(frq[:, 2, i : i + 1], c)
            tabs["pos"] = sbuf([P, 12, 64], F32, "tmp0", TMP)
            nc.gpsimd.iota(
                tabs["pos"][:], pattern=[[128, 12], [0, 64]], base=0, channel_multiplier=1,
                allow_small_or_imprecise_dtypes=True,
            )

        def tmp(j, dtype):
            return sbuf([P, 12, 64], dtype, "tmp%d" % j, TMP + 3 * j)

        def part(j):
            return tabs["frq"][:, j, :].unsqueeze(1).to_broadcast([P, 12, 64])

        def wrap(dst, src):
            nc.vector.scalar_tensor_tensor(out=dst[:], in0=src[:], scalar=0.5, in1=src[:], op0=ALU.is_gt, op1=ALU.subtract)

        def table_step(s):
            t = tabs
            if s == 0:
                t["u"] = tmp(1, F32)
                nc.vector.tensor_tensor(out=t["u"][:], in0=t["pos"][:], in1=part(0), op=ALU.mult)
            elif s == 1:
                t["ki"] = tmp(2, I32)
                nc.vector.tensor_copy(out=t["ki"][:], in_=t["u"][:])
            elif s == 2:
                t["kf"] = tmp(3, F32)
                nc.vector.tensor_copy(out=t["kf"][:], in_=t["ki"][:])
            elif s == 3:
                t["f"] = tmp(4, F32)
                nc.vector.tensor_tensor(out=t["f"][:], in0=t["u"][:], in1=t["kf"][:], op=ALU.subtract)
            elif s == 4:
                t["v"] = tmp(5, F32)
                nc.vector.tensor_tensor(out=t["v"][:], in0=t["pos"][:], in1=part(1), op=ALU.mult)
            elif s == 5:
                t["f2"] = tmp(6, F32)
                nc.vector.tensor_tensor(out=t["f2"][:], in0=t["f"][:], in1=t["v"][:], op=ALU.add)
            elif s == 6:
                t["v2"] = tmp(1, F32)
                nc.vector.tensor_tensor(out=t["v2"][:], in0=t["pos"][:], in1=part(2), op=ALU.mult)
            elif s == 7:
                t["f3"] = tmp(2, F32)
                nc.vector.tensor_tensor(out=t["f3"][:], in0=t["f2"][:], in1=t["v2"][:], op=ALU.add)
            elif s == 8:
                t["g1"] = tmp(3, F32)
                wrap(t["g1"], t["f3"])
            elif s == 9:
                t["fw"] = tmp(4, F32)
                wrap(t["fw"], t["g1"])
            elif s == 10:
                t["sin"] = sbuf([P, 12, 64], F32, "sin", TAB + 3)
                nc.scalar.activation(out=t["sin"][:], in_=t["fw"][:], func=ACT.Sin, scale=2.0 * PI)
                t["fc"] = tmp(5, F32)
                nc.vector.tensor_scalar_add(out=t["fc"][:], in0=t["fw"][:], scalar1=0.25)
            elif s == 11:
                t["gc"] = tmp(6, F32)
                wrap(t["gc"], t["fc"])
            elif s == 12:
                t["cos"] = sbuf([P, 12, 64], F32, "cos", TAB)
                nc.scalar.activation(out=t["cos"][:], in_=t["gc"][:], func=ACT.Sin, scale=-2.0 * PI)

        ident = sbuf([P, P], F32, "ident", IDENT)
        make_identity(nc, ident[:])

        load_x(0)
        load_x(1)
        load_w(0, 0)
        load_w(0, 1)
        load_x(2)
        load_w(0, 2)
        load_w(0, 3)

        acc = {}
        for k in range(26):
            if FIRST_SORTED <= k + 1 < 24:
                x_sort(k + 1)
            if k < 24:
                transpose_run(k)
                if k + 3 < 24 and k < FIRST_SORTED:
                    load_x(k + 3)
                if k == 0:
                    load_w(0, 4)
                x_copy(k)
                x_quant(k)
            if k >= 2:
                n, cp = divmod(k - 2, 4)
                if cp == 0:
                    for t in range(4):
                        acc[t] = bank(4 + t)
                for c in (2 * cp, 2 * cp + 1):
                    for t in range(4):
                        mx_first(acc[t], 0, n, t, c)
                if cp == 3:
                    for t in range(4):
                        ql_evac("S" if t % 2 == 0 else "V", n, t, acc[t])
            if 1 <= k <= 4:
                a = 2 * (k - 1)
                w_interleave("S", 0, a)
                w_interleave("V", 0, a + 1)
                w_quant(0, a)
                w_quant(0, a + 1)
                if a + 5 < 8:
                    load_w(0, a + 5)
                if a + 6 < 8:
                    load_w(0, a + 6)
                if k == 4:
                    load_w(1, 0)
                    load_w(1, 1)
            if 6 <= k < 22:
                c, step = divmod(k - 6, 4)
                if step == 0:
                    w_interleave("S", 1, c, 0, 64)
                if step == 1:
                    w_interleave("S", 1, c, 64, 128)
                    load_w(1, c + 2)
                if step == 2:
                    w_quant(1, c)
            if k == 24:
                w_interleave("S", 1, 4)
                w_interleave("V", 1, 5)
                load_w(1, 6)
                load_w(1, 7)
            if k == 25:
                w_quant(1, 4)
                w_quant(1, 5)

        table_constants()

        pair = {}
        for n in range(2):
            for t in range(4):
                pair[(n, t)] = next_bank()
        for c in range(8):
            if c == 0:
                w_interleave("S", 1, 6)
                w_interleave("V", 1, 7)
                load_w(2, 0)
                load_w(2, 1)
            for n in range(2):
                for t in range(4):
                    mx_first(pair[(n, t)], 1, n, t, c)
            if c == 1:
                w_quant(1, 6)
                w_quant(1, 7)
            if 1 <= c < 7:
                ql_quant(c - 1)
            if c < 6:
                ql_interleave(c)
        for n in range(2):
            for t in range(4):
                ql_evac("S" if t % 2 == 0 else "V", 6 + n, t, pair[(n, t)])
        ql_interleave(6)

        for g in range(1, 6):
            for n in range(2 if g == 1 else 0, 6):
                e = 6 * g + n
                for t in range(4):
                    pos = 4 * n + t - (8 if g == 1 else 0)
                    a = next_bank()
                    for c in range(8):
                        mx_first(a, g, n, t, c)
                    ql_evac("S", e, t, a)
                    if g < 5 and pos < 16:
                        c = pos // 2
                        if pos % 2 == 0:
                            w_interleave("S" if c % 2 == 0 else "V", g + 1, c)
                            if c + 2 < 8:
                                load_w(g + 1, c + 2)
                            elif g + 2 < 6:
                                load_w(g + 2, c - 6)
                        else:
                            w_quant(g + 1, c)
                    if g == 5:
                        if pos == 0:
                            load_b(0)
                            load_b(1)
                            load_b(2)
                        for u in range(12):
                            if pos == 4 + (3 * u) // 2:
                                b_copy(u, "S" if u % 2 == 0 else "V", "V")
                        for u in range(12):
                            if pos == 5 + (3 * u) // 2:
                                b_quant(u)
                    if e == 8 and t == 0:
                        ql_quant(6)
                    if t == 1:
                        ql_interleave(e - 1)
                    if t == 2:
                        ql_quant(e - 1)
                    if g == 2 and pos < 13:
                        table_step(pos)
        ql_interleave(35)
        ql_quant(35)

        outt, ra, rb = {}, {}, {}
        pending = []

        def rope_head(s, bk, a):
            x = 2 * s + bk
            pt = (s % 24) % 12
            xv = a[:].rearrange("p (h i two) -> p h two i", h=4, two=2)
            rb[x] = sbuf([P, 4, 2, 64], F32, "rb%d" % (x % 2), RTMP + 4 * (x % 2) + 2)
            sin3 = tabs["sin"][:, pt, :].unsqueeze(1).to_broadcast([P, 4, 64])
            nc.vector.scalar_tensor_tensor(
                out=rb[x][:, :, 0, :], in0=xv[:, :, 1, :], scalar=-1.0, in1=sin3, op0=ALU.mult, op1=ALU.mult
            )
            nc.vector.tensor_tensor(out=rb[x][:, :, 1, :], in0=xv[:, :, 0, :], in1=sin3, op=ALU.mult)
            rope_tail()
            ra[x] = sbuf([P, 4, 2, 64], F32, "ra%d" % (x % 2), RTMP + 4 * (x % 2))
            cos4 = tabs["cos"][:, pt, :].unsqueeze(1).unsqueeze(1).to_broadcast([P, 4, 2, 64])
            nc.vector.tensor_tensor(out=ra[x][:], in0=xv, in1=cos4, op=ALU.mult)
            pending.append((s, bk))

        def rope_tail():
            if len(pending) == 0:
                return
            s, bk = pending.pop(0)
            x = 2 * s + bk
            nc.vector.tensor_tensor(
                out=outt[s][:, 4 * bk : 4 * bk + 4, NOPE:HEAD].rearrange("p h (i two) -> p h i two", two=2),
                in0=ra[x][:].rearrange("p h two i -> p h i two"),
                in1=rb[x][:].rearrange("p h two i -> p h i two"),
                op=ALU.add,
            )
            if bk == 1:
                sc, tt = divmod(s, 24)
                b, p0 = divmod(128 * tt, SEQ)
                nc.scalar.dma_start(
                    out=out[b, 8 * sc : 8 * sc + 8, p0 : p0 + P, :].rearrange("h p d -> p h d"), in_=outt[s][:]
                )

        for s in range(48):
            sc, tt = divmod(s, 24)
            outt[s] = sbuf([P, 8, HEAD], F32, "outt%d" % (s % 3), OUTT + 6 * (s % 3))
            for bk in range(3):
                a = next_bank()
                for g2 in range(6):
                    k = 4 * (g2 % 4)
                    nc.tensor.matmul_mx(
                        out=a[:],
                        lhsT=ql_codes(g2, tt // 4)[:, 128 * (tt % 4) : 128 * (tt % 4 + 1)].bitcast(FP8X4),
                        lhsT_scale=qlpl[k:P, g2 // 4, 128 * tt : 128 * (tt + 1)],
                        rhs=bc[(sc, bk, g2)][:].bitcast(FP8X4),
                        rhs_scale=bpl[(sc, bk)][k:P, g2 // 4, :],
                        start=(g2 == 0),
                        stop=(g2 == 5),
                    )
                if bk < 2:
                    rope_head(s, bk, a)
                else:
                    nc.scalar.copy(out=outt[s][:, :, 0:NOPE], in_=a[:].rearrange("p (h r) -> p h r", h=8))
                if bk == 1 and sc == 0:
                    for u in range(12):
                        if tt == (5 * u) // 3:
                            b_copy(12 + u, "S", "S")
                    for u in range(12):
                        if tt == (5 * u) // 3 + 1:
                            b_quant(12 + u)
        rope_tail()
        rope_tail()
